import numpy as np
import ml_dtypes


def mxq(x, axis, fmt="e4m3"):
    dtype, down = {"e4m3": (ml_dtypes.float8_e4m3fn, 7), "e5m2": (ml_dtypes.float8_e5m2, 14)}[fmt]
    v = np.moveaxis(np.asarray(x, np.float32).astype(ml_dtypes.bfloat16).astype(np.float64), axis, -1)
    blocks = v.reshape(v.shape[:-1] + (-1, 32))
    amax = np.abs(blocks).max(-1, keepdims=True)
    byte = np.maximum(np.where(amax > 0, np.frexp(amax)[1] - 1 + 127, 0) - down, 1)
    scale = np.exp2(byte - 127.0)
    codes = (blocks / scale).astype(np.float32).astype(dtype).astype(np.float64)
    return np.moveaxis((codes * scale).reshape(v.shape), -1, axis)


WIDE = False


def mx_kscale(k):
    if not WIDE:
        return np.ones(k)
    levels = np.array([10, -10, 5, -5, 0])
    a = np.random.permutation(np.resize(levels, k // 512 * 4)).reshape(k // 512, 4)
    idx = np.arange(k)
    return np.exp2(a[idx // 512, idx % 128 // 32])


BF16 = ml_dtypes.bfloat16


def bf(x):
    return np.asarray(x, np.float32).astype(BF16)


def f64(x):
    return np.asarray(x).astype(np.float64)


E2M1 = np.array([0.0, 0.5, 1.0, 1.5, 2.0, 3.0, 4.0, 6.0, -0.0, -0.5, -1.0, -1.5, -2.0, -3.0, -4.0, -6.0])


def pack_weight(w, fmt):
    k, n = w.shape
    w = f64(bf(w)).reshape(k // 32, 32, n)
    amax = np.abs(w).max(1)
    if fmt == "e4m3":
        byte = np.frexp(amax)[1] - 1 + 127 - 7
    else:
        mant, ex = np.frexp(amax / 6.0)
        byte = np.where(mant > 0.5, ex, ex - 1) + 127
    byte = np.clip(np.where(amax > 0, byte, 1), 1, 254)
    scaled = (w * np.exp2(127.0 - byte)[:, None, :]).reshape(k, n).astype(np.float32)
    by_word = np.ascontiguousarray(scaled.reshape(k // 512, 128, 4, n).transpose(0, 1, 3, 2))
    if fmt == "e4m3":
        words = by_word.astype(ml_dtypes.float8_e4m3fn).view(np.uint8)
    else:
        c = by_word.astype(ml_dtypes.float4_e2m1fn).view(np.uint8) & 0xF
        words = c[..., 0::2] | (c[..., 1::2] << 4)
    return np.ascontiguousarray(words), np.ascontiguousarray(byte.astype(np.uint8).reshape(k // 512, 16, n))


def unpack_weight(words, scales, fmt):
    g, p, n, _ = words.shape
    if fmt == "e4m3":
        vals = np.ascontiguousarray(words).view(ml_dtypes.float8_e4m3fn).astype(np.float64)
    else:
        nib = np.empty((g, p, n, 4), np.uint8)
        nib[..., 0::2] = words & 0xF
        nib[..., 1::2] = words >> 4
        vals = E2M1[nib]
    vals = vals * np.repeat(np.exp2(scales.astype(np.float64) - 127.0), 8, axis=1)[..., None]
    return vals.transpose(0, 1, 3, 2).reshape(g * 512, n)


B, Q_LEN, CTX, HID, H, KVH, D = 2, 64, 128, 8192, 16, 4, 128
T = CTX + Q_LEN
EPS = 1e-6
ROPE_BASE = 10000.0


def rms_norm(x, w):
    return x * (1.0 / np.sqrt(np.mean(x * x, axis=-1, keepdims=True) + EPS)) * w


def rotate_half(x):
    h = x.shape[-1] // 2
    return np.concatenate([-x[..., h:], x[..., :h]], axis=-1)


def setup_inputs():
    s = mx_kscale(HID)
    inv_freq = 1.0 / ROPE_BASE ** (np.arange(0, D, 2) / D)
    pos = np.random.randint(0, CTX, size=(B, 1)) + np.arange(T)[None, :]
    ang = pos[:, :, None] * inv_freq
    emb = np.concatenate([ang, ang], axis=-1)
    hidden_states = bf(np.random.standard_normal((B, Q_LEN, HID)) * s)
    target_hidden = bf(np.random.standard_normal((B, CTX, HID)) * s)
    Wq_words, Wq_scales = pack_weight((np.random.standard_normal((H * D, HID)) / np.sqrt(HID) / s[None, :]).T, "e4m3")
    Wk_words, Wk_scales = pack_weight((np.random.standard_normal((KVH * D, HID)) / np.sqrt(HID) / s[None, :]).T, "e4m3")
    Wv_words, Wv_scales = pack_weight((np.random.standard_normal((KVH * D, HID)) * 2.0 / np.sqrt(HID) / s[None, :]).T, "e4m3")
    return {"hidden_states": hidden_states,
            "target_hidden": target_hidden,
            "cos": bf(np.cos(emb)),
            "sin": bf(np.sin(emb)),
            "Wq_words": Wq_words,
            "Wq_scales": Wq_scales,
            "Wk_words": Wk_words,
            "Wk_scales": Wk_scales,
            "Wv_words": Wv_words,
            "Wv_scales": Wv_scales,
            "q_norm_w": bf(1.0 + 0.1 * np.random.standard_normal(D)),
            "k_norm_w": bf(1.0 + 0.1 * np.random.standard_normal(D))}


def reference(hidden_states, target_hidden, cos, sin, Wq_words, Wq_scales, Wk_words, Wk_scales, Wv_words, Wv_scales, q_norm_w, k_norm_w):
    kv_in = mxq(np.concatenate([f64(target_hidden), f64(hidden_states)], axis=1), 2, "e4m3")
    h_in = kv_in[:, CTX:, :]
    q = (h_in @ unpack_weight(Wq_words, Wq_scales, "e4m3")).reshape(B, Q_LEN, H, D)
    q = rms_norm(q, f64(q_norm_w)).transpose(0, 2, 1, 3)
    k = (kv_in @ unpack_weight(Wk_words, Wk_scales, "e4m3")).reshape(B, T, KVH, D)
    k = rms_norm(k, f64(k_norm_w)).transpose(0, 2, 1, 3)
    v = (kv_in @ unpack_weight(Wv_words, Wv_scales, "e4m3")).reshape(B, T, KVH, D).transpose(0, 2, 1, 3)
    c = f64(cos)[:, None, :, :]
    s = f64(sin)[:, None, :, :]
    q = q * c[:, :, -Q_LEN:, :] + rotate_half(q) * s[:, :, -Q_LEN:, :]
    k = k * c + rotate_half(k) * s
    return q, k, v

@@ -1,0 +1,260 @@
+import concourse.mybir as mybir
+from concourse.masks import make_identity
+
+F32 = mybir.dt.float32
+BF16 = mybir.dt.bfloat16
+I32 = mybir.dt.int32
+U32 = mybir.dt.uint32
+U8 = mybir.dt.uint8
+FP8X4 = mybir.dt.float8_e4m3fn_x4
+MULT = mybir.AluOpType.mult
+ADD = mybir.AluOpType.add
+ACT = mybir.ActivationFunctionType
+
+P = 128
+BATCH, Q_LEN, CTX, HID, HEADS, KV_HEADS, D = 2, 64, 128, 8192, 16, 4, 128
+T = CTX + Q_LEN
+HALF = D // 2
+EPS = 1e-6
+K_PASS = 512
+GROUPS = HID // K_PASS
+N_PASS = 512
+HEADS_PER_BANK = N_PASS // D
+TOKEN_TILES = 3
+NEW_TOKENS = 2
+SHARE = 4
+X_CHUNK_GROUPS = 8
+QUANT_GROUPS = 4
+BANK_GROUPS = 2
+Q_WIDE = 3 * N_PASS
+
+FLOPS = 2 * HID * (BATCH * Q_LEN * HEADS * D + 2 * BATCH * T * KV_HEADS * D)
+
+
+def zeroed_scale_planes(nc, pool, width, name):
+    planes = pool.tile([P, GROUPS // SHARE, width], U8, name=name, align_bytes=64)
+    nc.vector.memset(planes[:].rearrange("p a n -> p (a n)").bitcast(I32), 0)
+    return planes
+
+
+def load_scale_planes(nc, planes, scales):
+    for a in range(GROUPS // SHARE):
+        for quadrant in range(4):
+            nc.sync.dma_start(
+                out=planes[32 * quadrant : 32 * quadrant + 4 * SHARE, a, :].bitcast(I32),
+                in_=scales[SHARE * a : SHARE * (a + 1), 4 * quadrant : 4 * quadrant + 4, :].bitcast(I32),
+            )
+
+
+def plane_of(planes, g, columns):
+    return planes[4 * (g % SHARE) : P, g // SHARE, columns]
+
+
+def tile_dflashattention_pa_k_kernel(
+    tc,
+    hidden_states,
+    target_hidden,
+    cos,
+    sin,
+    Wq_words,
+    Wq_scales,
+    Wk_words,
+    Wk_scales,
+    Wv_words,
+    Wv_scales,
+    q_norm_w,
+    k_norm_w,
+    out_q,
+    out_k,
+    out_v,
+):
+    nc = tc.nc
+    x_tiles = [target_hidden[0], target_hidden[1], hidden_states.rearrange("b t k -> (b t) k")]
+
+    with tc.tile_pool(name="keep", bufs=1) as keep, tc.tile_pool(name="narrow", bufs=8) as narrow:
+        ident = keep.tile([P, P], F32)
+        make_identity(nc, ident[:])
+        k_planes = zeroed_scale_planes(nc, keep, N_PASS, "k_planes")
+        v_planes = zeroed_scale_planes(nc, keep, N_PASS, "v_planes")
+        q_planes = zeroed_scale_planes(nc, keep, HEADS * D, "q_planes")
+        turned = keep.tile([P, 2, D], F32)
+        direct_tab = keep.tile([P, TOKEN_TILES + 1, D], F32)
+        crossed_tab = keep.tile([P, TOKEN_TILES + 1, D], F32)
+
+        cos_sb = keep.tile([P, TOKEN_TILES, D], BF16)
+        sin_sb = keep.tile([P, TOKEN_TILES, D], BF16)
+        for table, table_sb in ((cos, cos_sb), (sin, sin_sb)):
+            nc.scalar.dma_start(out=table_sb[:, 0:BATCH, :], in_=table[:, 0:CTX, :].rearrange("b t d -> t b d"))
+            for b in range(BATCH):
+                nc.scalar.dma_start(
+                    out=table_sb[Q_LEN * b : Q_LEN * (b + 1), NEW_TOKENS, :], in_=table[b, CTX:T, :]
+                )
+        gain = keep.tile([P, 2, D], BF16)
+        nc.scalar.dma_start(out=gain[:, 0, :], in_=k_norm_w.partition_broadcast(P))
+        nc.scalar.dma_start(out=gain[:, 1, :], in_=q_norm_w.partition_broadcast(P))
+
+        x_codes = keep.tile([P, TOKEN_TILES, GROUPS, P], U32, align_bytes=64)
+        x_scales = keep.tile([P, TOKEN_TILES, GROUPS, P], U8, align_bytes=64)
+        with tc.tile_pool(name="x_raw", bufs=6) as x_raw, tc.tile_pool(name="stage", bufs=4) as stage, tc.psum_pool(name="flip", bufs=8) as flip:
+            for chunk in range(GROUPS // X_CHUNK_GROUPS):
+                for tile_i in range(TOKEN_TILES):
+                    raw = x_raw.tile([P, X_CHUNK_GROUPS * K_PASS], BF16)
+                    k0 = chunk * X_CHUNK_GROUPS * K_PASS
+                    nc.sync.dma_start(out=raw[:], in_=x_tiles[tile_i][:, k0 : k0 + X_CHUNK_GROUPS * K_PASS])
+                    pairs = raw[:].bitcast(F32)
+                    pairs_per_group = K_PASS // 2
+                    for part in range(X_CHUNK_GROUPS // QUANT_GROUPS):
+                        grouped = stage.tile([P, QUANT_GROUPS, P, 4], BF16, align_bytes=64)
+                        for bank in range(QUANT_GROUPS // BANK_GROUPS):
+                            flipped = flip.tile([P, BANK_GROUPS, 2, P], F32)
+                            for j in range(BANK_GROUPS):
+                                first = (part * QUANT_GROUPS + bank * BANK_GROUPS + j) * pairs_per_group
+                                for u in range(2):
+                                    nc.tensor.transpose(
+                                        flipped[:, j, u, :],
+                                        pairs[:, first + u : first + pairs_per_group : 2],
+                                        ident[:],
+                                    )
+                            dst = grouped[:, bank * BANK_GROUPS : (bank + 1) * BANK_GROUPS, :, :].bitcast(F32)
+                            src = flipped[:].rearrange("p j u r -> p j r u")
+                            if (part * (QUANT_GROUPS // BANK_GROUPS) + bank) % 4 == 3:
+                                nc.vector.tensor_copy(out=dst, in_=src)
+                            else:
+                                nc.scalar.copy(out=dst, in_=src)
+                        g0 = chunk * X_CHUNK_GROUPS + part * QUANT_GROUPS
+                        nc.vector.quantize_mx(
+                            out=x_codes[:, tile_i, g0 : g0 + QUANT_GROUPS, :].rearrange("p g r -> p (g r)").bitcast(FP8X4),
+                            scales=x_scales[:, tile_i, g0 : g0 + QUANT_GROUPS, :].rearrange("p g r -> p (g r)"),
+                            in_=grouped[:].rearrange("p g r t -> p (g r t)"),
+                        )
+
+        load_scale_planes(nc, k_planes, Wk_scales)
+        load_scale_planes(nc, v_planes, Wv_scales)
+        load_scale_planes(nc, q_planes, Wq_scales)
+
+        nc.vector.tensor_scalar_mul(out=turned[:, :, 0:HALF], in0=gain[:, :, HALF:D], scalar1=-1.0)
+        nc.vector.tensor_copy(out=turned[:, :, HALF:D], in_=gain[:, :, 0:HALF])
+        for tab, angle, weight in ((direct_tab, cos_sb, gain), (crossed_tab, sin_sb, turned)):
+            nc.vector.tensor_tensor(
+                out=tab[:, 0:TOKEN_TILES, :],
+                in0=angle[:],
+                in1=weight[:, 0, :].unsqueeze(1).to_broadcast([P, TOKEN_TILES, D]),
+                op=MULT,
+            )
+            nc.vector.tensor_tensor(
+                out=tab[:, TOKEN_TILES, :], in0=angle[:, NEW_TOKENS, :], in1=weight[:, 1, :], op=MULT
+            )
+
+        with tc.tile_pool(name="wide", bufs=8) as wide, tc.tile_pool(name="after", bufs=3) as after, tc.psum_pool(name="sums", bufs=8) as sums:
+
+            def project(acc, tile_i, g, words, planes, columns):
+                nc.tensor.matmul_mx(
+                    out=acc[:],
+                    lhsT=x_codes[:, tile_i, g, :].bitcast(FP8X4),
+                    lhsT_scale=x_scales[:, tile_i, g, :],
+                    rhs=words.bitcast(FP8X4),
+                    rhs_scale=plane_of(planes, g, columns),
+                    start=(g == 0),
+                    stop=(g == GROUPS - 1),
+                )
+
+            def norm_and_rotate(acc, table):
+                shape = [P, HEADS_PER_BANK, D]
+                half_shape = [P, HEADS_PER_BANK, HALF]
+                u = after.tile(shape, F32, name="u")
+                nc.scalar.copy(out=u[:].rearrange("p h d -> p (h d)"), in_=acc[:])
+                squares = after.tile(shape, F32, name="squares")
+                sum_sq = after.tile([P, HEADS_PER_BANK], F32, name="sum_sq")
+                for h in range(HEADS_PER_BANK):
+                    nc.scalar.activation(
+                        out=squares[:, h, :], in_=u[:, h, :], func=ACT.Square, accum_out=sum_sq[:, h : h + 1]
+                    )
+                rms = after.tile([P, HEADS_PER_BANK], F32, name="rms")
+                nc.scalar.activation(out=rms[:], in_=sum_sq[:], func=ACT.Sqrt, scale=1.0 / D, bias=EPS)
+                rstd = after.tile([P, HEADS_PER_BANK], F32, name="rstd")
+                nc.vector.reciprocal(out=rstd[:], in_=rms[:])
+                res = after.tile(shape, F32, name="res")
+                nc.vector.tensor_tensor(
+                    out=res[:], in0=u[:], in1=direct_tab[:, table, :].unsqueeze(1).to_broadcast(shape), op=MULT
+                )
+                crossed = after.tile(shape, F32, name="crossed")
+                nc.vector.tensor_tensor(
+                    out=crossed[:, :, 0:HALF],
+                    in0=u[:, :, HALF:D],
+                    in1=crossed_tab[:, table, 0:HALF].unsqueeze(1).to_broadcast(half_shape),
+                    op=MULT,
+                )
+                nc.vector.tensor_tensor(
+                    out=crossed[:, :, HALF:D],
+                    in0=u[:, :, 0:HALF],
+                    in1=crossed_tab[:, table, HALF:D].unsqueeze(1).to_broadcast(half_shape),
+                    op=MULT,
+                )
+                nc.vector.tensor_tensor(out=res[:], in0=res[:], in1=crossed[:], op=ADD)
+                nc.vector.tensor_tensor(
+                    out=res[:], in0=res[:], in1=rstd[:].unsqueeze(2).to_broadcast(shape), op=MULT
+                )
+                return res
+
+            def store_new_tokens(queue, out, heads, first_token, res):
+                for b in range(BATCH):
+                    queue.dma_start(
+                        out=out[b, heads, first_token : first_token + Q_LEN, :].rearrange("h t d -> t h d"),
+                        in_=res[Q_LEN * b : Q_LEN * (b + 1), :, :],
+                    )
+
+            def store_kv(out, tile_i, res):
+                if tile_i == NEW_TOKENS:
+                    store_new_tokens(nc.gpsimd, out, slice(0, KV_HEADS), CTX, res)
+                else:
+                    nc.gpsimd.dma_start(out=out[tile_i, :, 0:CTX, :].rearrange("h t d -> t h d"), in_=res[:])
+
+            v_acc = [sums.tile([P, N_PASS], F32, name="v_acc%d" % i, tag="acc") for i in range(TOKEN_TILES)]
+            k_acc = [sums.tile([P, N_PASS], F32, name="k_acc%d" % i, tag="acc") for i in range(TOKEN_TILES)]
+            for a in range(GROUPS // SHARE):
+                loaded = []
+                for words_in in (Wv_words, Wk_words):
+                    words = narrow.tile([P, SHARE, N_PASS], U32, name="words", tag="narrow", align_bytes=64)
+                    nc.sync.dma_start(
+                        out=words[:].bitcast(I32),
+                        in_=words_in[SHARE * a : SHARE * (a + 1)].rearrange("g p n t -> p g (n t)").bitcast(I32),
+                    )
+                    loaded.append(words)
+                for i in range(SHARE):
+                    g = SHARE * a + i
+                    for tile_i in range(TOKEN_TILES):
+                        project(v_acc[tile_i], tile_i, g, loaded[0][:, i, :], v_planes, slice(0, N_PASS))
+                        project(k_acc[tile_i], tile_i, g, loaded[1][:, i, :], k_planes, slice(0, N_PASS))
+            for tile_i in range(TOKEN_TILES):
+                v_sb = after.tile([P, KV_HEADS, D], F32, name="v_sb")
+                nc.vector.tensor_copy(out=v_sb[:].rearrange("p h d -> p (h d)"), in_=v_acc[tile_i][:])
+                store_kv(out_v, tile_i, v_sb)
+            for tile_i in range(TOKEN_TILES):
+                store_kv(out_k, tile_i, norm_and_rotate(k_acc[tile_i], tile_i))
+
+            wide_banks = Q_WIDE // N_PASS
+            q_acc = [sums.tile([P, N_PASS], F32, name="q_acc%d" % j, tag="acc") for j in range(wide_banks + 1)]
+            for g in range(GROUPS):
+                words = wide.tile([P, Q_WIDE], U32, name="wide_words", align_bytes=64)
+                nc.sync.dma_start(
+                    out=words[:].bitcast(I32),
+                    in_=Wq_words[g].rearrange("p n t -> p (n t)")[:, 0 : 4 * Q_WIDE].bitcast(I32),
+                )
+                for j in range(wide_banks):
+                    columns = slice(N_PASS * j, N_PASS * (j + 1))
+                    project(q_acc[j], NEW_TOKENS, g, words[:, columns], q_planes, columns)
+            for a in range(GROUPS // SHARE):
+                words = narrow.tile([P, SHARE, N_PASS], U32, name="words", tag="narrow", align_bytes=64)
+                nc.sync.dma_start(
+                    out=words[:].bitcast(I32),
+                    in_=Wq_words[SHARE * a : SHARE * (a + 1), :, Q_WIDE : HEADS * D, :]
+                    .rearrange("g p n t -> p g (n t)")
+                    .bitcast(I32),
+                )
+                for i in range(SHARE):
+                    project(
+                        q_acc[wide_banks], NEW_TOKENS, SHARE * a + i, words[:, i, :], q_planes, slice(Q_WIDE, HEADS * D)
+                    )
+            for j in range(wide_banks + 1):
+                res = norm_and_rotate(q_acc[j], TOKEN_TILES)
+                store_new_tokens(nc.sync, out_q, slice(HEADS_PER_BANK * j, HEADS_PER_BANK * (j + 1)), 0, res)

@@ -23,6 +23,7 @@ HEADS_PER_BANK = N_PASS // D
 TOKEN_TILES = 3
 NEW_TOKENS = 2
 SHARE = 4
+K_OFFSET, V_OFFSET = 0, 4
 X_CHUNK_GROUPS = 8
 QUANT_GROUPS = 4
 BANK_GROUPS = 2
@@ -31,23 +32,10 @@ Q_WIDE = 3 * N_PASS
 FLOPS = 2 * HID * (BATCH * Q_LEN * HEADS * D + 2 * BATCH * T * KV_HEADS * D)
 
 
-def zeroed_scale_planes(nc, pool, width, name):
-    planes = pool.tile([P, GROUPS // SHARE, width], U8, name=name, align_bytes=64)
+def zeroed_bytes(nc, pool, shape, name):
+    planes = pool.tile(shape, U8, name=name, align_bytes=64)
     nc.vector.memset(planes[:].rearrange("p a n -> p (a n)").bitcast(I32), 0)
     return planes
-
-
-def load_scale_planes(nc, planes, scales):
-    for a in range(GROUPS // SHARE):
-        for quadrant in range(4):
-            nc.sync.dma_start(
-                out=planes[32 * quadrant : 32 * quadrant + 4 * SHARE, a, :].bitcast(I32),
-                in_=scales[SHARE * a : SHARE * (a + 1), 4 * quadrant : 4 * quadrant + 4, :].bitcast(I32),
-            )
-
-
-def plane_of(planes, g, columns):
-    return planes[4 * (g % SHARE) : P, g // SHARE, columns]
 
 
 def tile_dflashattention_pa_k_kernel(
@@ -74,9 +62,22 @@ def tile_dflashattention_pa_k_kernel(
     with tc.tile_pool(name="keep", bufs=1) as keep, tc.tile_pool(name="narrow", bufs=8) as narrow:
         ident = keep.tile([P, P], F32)
         make_identity(nc, ident[:])
-        k_planes = zeroed_scale_planes(nc, keep, N_PASS, "k_planes")
-        v_planes = zeroed_scale_planes(nc, keep, N_PASS, "v_planes")
-        q_planes = zeroed_scale_planes(nc, keep, HEADS * D, "q_planes")
+
+        kv_planes = zeroed_bytes(nc, keep, [P, GROUPS, N_PASS], "kv_planes")
+        q_planes = zeroed_bytes(nc, keep, [P, GROUPS // SHARE, HEADS * D], "q_planes")
+        for r in range(4):
+            for offset, scales in ((K_OFFSET, Wk_scales), (V_OFFSET, Wv_scales)):
+                nc.gpsimd.dma_start(
+                    out=kv_planes[offset + r : P : 32, :, :].bitcast(F32),
+                    in_=scales[:, r : 16 : 4, :].rearrange("g q n -> q g n").bitcast(F32),
+                )
+        for a in range(GROUPS // SHARE):
+            for quadrant in range(4):
+                nc.gpsimd.dma_start(
+                    out=q_planes[32 * quadrant : 32 * quadrant + 4 * SHARE, a, :].bitcast(F32),
+                    in_=Wq_scales[SHARE * a : SHARE * (a + 1), 4 * quadrant : 4 * quadrant + 4, :].bitcast(F32),
+                )
+
         turned = keep.tile([P, 2, D], F32)
         direct_tab = keep.tile([P, TOKEN_TILES + 1, D], F32)
         crossed_tab = keep.tile([P, TOKEN_TILES + 1, D], F32)
@@ -128,10 +129,6 @@ def tile_dflashattention_pa_k_kernel(
                             in_=grouped[:].rearrange("p g r t -> p (g r t)"),
                         )
 
-        load_scale_planes(nc, k_planes, Wk_scales)
-        load_scale_planes(nc, v_planes, Wv_scales)
-        load_scale_planes(nc, q_planes, Wq_scales)
-
         nc.vector.tensor_scalar_mul(out=turned[:, :, 0:HALF], in0=gain[:, :, HALF:D], scalar1=-1.0)
         nc.vector.tensor_copy(out=turned[:, :, HALF:D], in_=gain[:, :, 0:HALF])
         for tab, angle, weight in ((direct_tab, cos_sb, gain), (crossed_tab, sin_sb, turned)):
@@ -145,18 +142,21 @@ def tile_dflashattention_pa_k_kernel(
                 out=tab[:, TOKEN_TILES, :], in0=angle[:, NEW_TOKENS, :], in1=weight[:, 1, :], op=MULT
             )
 
-        with tc.tile_pool(name="wide", bufs=8) as wide, tc.tile_pool(name="after", bufs=3) as after, tc.psum_pool(name="sums", bufs=8) as sums:
+        with tc.tile_pool(name="wide", bufs=10) as wide, tc.tile_pool(name="after", bufs=3) as after, tc.psum_pool(name="sums", bufs=8) as sums:
 
-            def project(acc, tile_i, g, words, planes, columns):
+            def project(acc, tile_i, g, words, plane):
                 nc.tensor.matmul_mx(
                     out=acc[:],
                     lhsT=x_codes[:, tile_i, g, :].bitcast(FP8X4),
                     lhsT_scale=x_scales[:, tile_i, g, :],
                     rhs=words.bitcast(FP8X4),
-                    rhs_scale=plane_of(planes, g, columns),
+                    rhs_scale=plane,
                     start=(g == 0),
                     stop=(g == GROUPS - 1),
                 )
+
+            def q_plane(g, columns):
+                return q_planes[4 * (g % SHARE) : P, g // SHARE, columns]
 
             def norm_and_rotate(acc, table):
                 shape = [P, HEADS_PER_BANK, D]
@@ -223,8 +223,8 @@ def tile_dflashattention_pa_k_kernel(
                 for i in range(SHARE):
                     g = SHARE * a + i
                     for tile_i in range(TOKEN_TILES):
-                        project(v_acc[tile_i], tile_i, g, loaded[0][:, i, :], v_planes, slice(0, N_PASS))
-                        project(k_acc[tile_i], tile_i, g, loaded[1][:, i, :], k_planes, slice(0, N_PASS))
+                        project(v_acc[tile_i], tile_i, g, loaded[0][:, i, :], kv_planes[V_OFFSET:P, g, :])
+                        project(k_acc[tile_i], tile_i, g, loaded[1][:, i, :], kv_planes[K_OFFSET:P, g, :])
             for tile_i in range(TOKEN_TILES):
                 v_sb = after.tile([P, KV_HEADS, D], F32, name="v_sb")
                 nc.vector.tensor_copy(out=v_sb[:].rearrange("p h d -> p (h d)"), in_=v_acc[tile_i][:])
@@ -242,7 +242,7 @@ def tile_dflashattention_pa_k_kernel(
                 )
                 for j in range(wide_banks):
                     columns = slice(N_PASS * j, N_PASS * (j + 1))
-                    project(q_acc[j], NEW_TOKENS, g, words[:, columns], q_planes, columns)
+                    project(q_acc[j], NEW_TOKENS, g, words[:, columns], q_plane(g, columns))
             for a in range(GROUPS // SHARE):
                 words = narrow.tile([P, SHARE, N_PASS], U32, name="words", tag="narrow", align_bytes=64)
                 nc.sync.dma_start(
@@ -252,9 +252,8 @@ def tile_dflashattention_pa_k_kernel(
                     .bitcast(I32),
                 )
                 for i in range(SHARE):
-                    project(
-                        q_acc[wide_banks], NEW_TOKENS, SHARE * a + i, words[:, i, :], q_planes, slice(Q_WIDE, HEADS * D)
-                    )
+                    g = SHARE * a + i
+                    project(q_acc[wide_banks], NEW_TOKENS, g, words[:, i, :], q_plane(g, slice(Q_WIDE, HEADS * D)))
             for j in range(wide_banks + 1):
                 res = norm_and_rotate(q_acc[j], TOKEN_TILES)
                 store_new_tokens(nc.sync, out_q, slice(HEADS_PER_BANK * j, HEADS_PER_BANK * (j + 1)), 0, res)

@@ -26,6 +26,7 @@ SHARE = 4
 K_OFFSET, V_OFFSET = 0, 4
 X_CHUNK_GROUPS = 8
 QUANT_GROUPS = 4
+LEAD_LOADS = 2
 BANK_GROUPS = 2
 Q_WIDE = 3 * N_PASS
 
@@ -65,12 +66,15 @@ def tile_dflashattention_pa_k_kernel(
 
         kv_planes = zeroed_bytes(nc, keep, [P, GROUPS, N_PASS], "kv_planes")
         q_planes = zeroed_bytes(nc, keep, [P, GROUPS // SHARE, HEADS * D], "q_planes")
-        for r in range(4):
-            for offset, scales in ((K_OFFSET, Wk_scales), (V_OFFSET, Wv_scales)):
-                nc.gpsimd.dma_start(
-                    out=kv_planes[offset + r : P : 32, :, :].bitcast(F32),
-                    in_=scales[:, r : 16 : 4, :].rearrange("g q n -> q g n").bitcast(F32),
-                )
+
+        def load_kv_scales():
+            for r in range(4):
+                for offset, scales in ((K_OFFSET, Wk_scales), (V_OFFSET, Wv_scales)):
+                    nc.sync.dma_start(
+                        out=kv_planes[offset + r : P : 32, :, :].bitcast(I32),
+                        in_=scales[:, r : 16 : 4, :].rearrange("g q n -> q g n").bitcast(I32),
+                    )
+
         for a in range(GROUPS // SHARE):
             for quadrant in range(4):
                 nc.gpsimd.dma_start(
@@ -85,23 +89,30 @@ def tile_dflashattention_pa_k_kernel(
         cos_sb = keep.tile([P, TOKEN_TILES, D], BF16)
         sin_sb = keep.tile([P, TOKEN_TILES, D], BF16)
         for table, table_sb in ((cos, cos_sb), (sin, sin_sb)):
-            nc.scalar.dma_start(out=table_sb[:, 0:BATCH, :], in_=table[:, 0:CTX, :].rearrange("b t d -> t b d"))
+            nc.gpsimd.dma_start(out=table_sb[:, 0:BATCH, :], in_=table[:, 0:CTX, :].rearrange("b t d -> t b d"))
             for b in range(BATCH):
-                nc.scalar.dma_start(
+                nc.gpsimd.dma_start(
                     out=table_sb[Q_LEN * b : Q_LEN * (b + 1), NEW_TOKENS, :], in_=table[b, CTX:T, :]
                 )
         gain = keep.tile([P, 2, D], BF16)
-        nc.scalar.dma_start(out=gain[:, 0, :], in_=k_norm_w.partition_broadcast(P))
-        nc.scalar.dma_start(out=gain[:, 1, :], in_=q_norm_w.partition_broadcast(P))
+        nc.gpsimd.dma_start(out=gain[:, 0, :], in_=k_norm_w.partition_broadcast(P))
+        nc.gpsimd.dma_start(out=gain[:, 1, :], in_=q_norm_w.partition_broadcast(P))
 
         x_codes = keep.tile([P, TOKEN_TILES, GROUPS, P], U32, align_bytes=64)
         x_scales = keep.tile([P, TOKEN_TILES, GROUPS, P], U8, align_bytes=64)
         with tc.tile_pool(name="x_raw", bufs=6) as x_raw, tc.tile_pool(name="stage", bufs=4) as stage, tc.psum_pool(name="flip", bufs=8) as flip:
+            raws = []
             for chunk in range(GROUPS // X_CHUNK_GROUPS):
                 for tile_i in range(TOKEN_TILES):
-                    raw = x_raw.tile([P, X_CHUNK_GROUPS * K_PASS], BF16)
+                    raw = x_raw.tile([P, X_CHUNK_GROUPS * K_PASS], BF16, name="raw")
                     k0 = chunk * X_CHUNK_GROUPS * K_PASS
                     nc.sync.dma_start(out=raw[:], in_=x_tiles[tile_i][:, k0 : k0 + X_CHUNK_GROUPS * K_PASS])
+                    raws.append(raw)
+                    if len(raws) == LEAD_LOADS:
+                        load_kv_scales()
+            for chunk in range(GROUPS // X_CHUNK_GROUPS):
+                for tile_i in range(TOKEN_TILES):
+                    raw = raws[chunk * TOKEN_TILES + tile_i]
                     pairs = raw[:].bitcast(F32)
                     pairs_per_group = K_PASS // 2
                     for part in range(X_CHUNK_GROUPS // QUANT_GROUPS):
@@ -142,7 +153,7 @@ def tile_dflashattention_pa_k_kernel(
                 out=tab[:, TOKEN_TILES, :], in0=angle[:, NEW_TOKENS, :], in1=weight[:, 1, :], op=MULT
             )
 
-        with tc.tile_pool(name="wide", bufs=10) as wide, tc.tile_pool(name="after", bufs=3) as after, tc.psum_pool(name="sums", bufs=8) as sums:
+        with tc.tile_pool(name="wide", bufs=12) as wide, tc.tile_pool(name="after", bufs=3) as after, tc.psum_pool(name="sums", bufs=8) as sums:
 
             def project(acc, tile_i, g, words, plane):
                 nc.tensor.matmul_mx(

@@ -26,7 +26,7 @@ SHARE = 4
 K_OFFSET, V_OFFSET = 0, 4
 X_CHUNK_GROUPS = 8
 QUANT_GROUPS = 4
-LEAD_LOADS = 2
+SMALL_PER_BIG = 3
 BANK_GROUPS = 2
 Q_WIDE = 3 * N_PASS
 
@@ -60,21 +60,22 @@ def tile_dflashattention_pa_k_kernel(
     nc = tc.nc
     x_tiles = [target_hidden[0], target_hidden[1], hidden_states.rearrange("b t k -> (b t) k")]
 
-    with tc.tile_pool(name="keep", bufs=1) as keep, tc.tile_pool(name="narrow", bufs=8) as narrow:
+    with tc.tile_pool(name="keep", bufs=1) as keep, tc.tile_pool(name="narrow", bufs=8) as narrow, tc.manual_schedule():
         ident = keep.tile([P, P], F32)
         make_identity(nc, ident[:])
 
         kv_planes = zeroed_bytes(nc, keep, [P, GROUPS, N_PASS], "kv_planes")
         q_planes = zeroed_bytes(nc, keep, [P, GROUPS // SHARE, HEADS * D], "q_planes")
 
-        def load_kv_scales():
-            for r in range(4):
-                for offset, scales in ((K_OFFSET, Wk_scales), (V_OFFSET, Wv_scales)):
-                    nc.sync.dma_start(
-                        out=kv_planes[offset + r : P : 32, :, :].bitcast(I32),
-                        in_=scales[:, r : 16 : 4, :].rearrange("g q n -> q g n").bitcast(I32),
+        small_loads = []
+        for r in range(4):
+            for offset, scales in ((K_OFFSET, Wk_scales), (V_OFFSET, Wv_scales)):
+                small_loads.append(
+                    (
+                        kv_planes[offset + r : P : 32, :, :].bitcast(I32),
+                        scales[:, r : 16 : 4, :].rearrange("g q n -> q g n").bitcast(I32),
                     )
-
+                )
         for a in range(GROUPS // SHARE):
             for quadrant in range(4):
                 nc.gpsimd.dma_start(
@@ -88,15 +89,13 @@ def tile_dflashattention_pa_k_kernel(
 
         cos_sb = keep.tile([P, TOKEN_TILES, D], BF16)
         sin_sb = keep.tile([P, TOKEN_TILES, D], BF16)
-        for table, table_sb in ((cos, cos_sb), (sin, sin_sb)):
-            nc.gpsimd.dma_start(out=table_sb[:, 0:BATCH, :], in_=table[:, 0:CTX, :].rearrange("b t d -> t b d"))
-            for b in range(BATCH):
-                nc.gpsimd.dma_start(
-                    out=table_sb[Q_LEN * b : Q_LEN * (b + 1), NEW_TOKENS, :], in_=table[b, CTX:T, :]
-                )
         gain = keep.tile([P, 2, D], BF16)
-        nc.gpsimd.dma_start(out=gain[:, 0, :], in_=k_norm_w.partition_broadcast(P))
-        nc.gpsimd.dma_start(out=gain[:, 1, :], in_=q_norm_w.partition_broadcast(P))
+        for table, table_sb in ((cos, cos_sb), (sin, sin_sb)):
+            small_loads.append((table_sb[:, 0:BATCH, :], table[:, 0:CTX, :].rearrange("b t d -> t b d")))
+            for b in range(BATCH):
+                small_loads.append((table_sb[Q_LEN * b : Q_LEN * (b + 1), NEW_TOKENS, :], table[b, CTX:T, :]))
+        small_loads.append((gain[:, 0, :], k_norm_w.partition_broadcast(P)))
+        small_loads.append((gain[:, 1, :], q_norm_w.partition_broadcast(P)))
 
         x_codes = keep.tile([P, TOKEN_TILES, GROUPS, P], U32, align_bytes=64)
         x_scales = keep.tile([P, TOKEN_TILES, GROUPS, P], U8, align_bytes=64)
@@ -107,9 +106,19 @@ def tile_dflashattention_pa_k_kernel(
                     raw = x_raw.tile([P, X_CHUNK_GROUPS * K_PASS], BF16, name="raw")
                     k0 = chunk * X_CHUNK_GROUPS * K_PASS
                     nc.sync.dma_start(out=raw[:], in_=x_tiles[tile_i][:, k0 : k0 + X_CHUNK_GROUPS * K_PASS])
+                    for sbuf_side, hbm_side in small_loads[SMALL_PER_BIG * len(raws) : SMALL_PER_BIG * (len(raws) + 1)]:
+                        nc.sync.dma_start(out=sbuf_side, in_=hbm_side)
                     raws.append(raw)
-                    if len(raws) == LEAD_LOADS:
-                        load_kv_scales()
+            assert SMALL_PER_BIG * len(raws) >= len(small_loads)
+
+            def quantise(grouped, tile_i, g0):
+                nc.vector.quantize_mx(
+                    out=x_codes[:, tile_i, g0 : g0 + QUANT_GROUPS, :].rearrange("p g r -> p (g r)").bitcast(FP8X4),
+                    scales=x_scales[:, tile_i, g0 : g0 + QUANT_GROUPS, :].rearrange("p g r -> p (g r)"),
+                    in_=grouped[:].rearrange("p g r t -> p (g r t)"),
+                )
+
+            waiting = []
             for chunk in range(GROUPS // X_CHUNK_GROUPS):
                 for tile_i in range(TOKEN_TILES):
                     raw = raws[chunk * TOKEN_TILES + tile_i]
@@ -133,25 +142,11 @@ def tile_dflashattention_pa_k_kernel(
                                 nc.vector.tensor_copy(out=dst, in_=src)
                             else:
                                 nc.scalar.copy(out=dst, in_=src)
-                        g0 = chunk * X_CHUNK_GROUPS + part * QUANT_GROUPS
-                        nc.vector.quantize_mx(
-                            out=x_codes[:, tile_i, g0 : g0 + QUANT_GROUPS, :].rearrange("p g r -> p (g r)").bitcast(FP8X4),
-                            scales=x_scales[:, tile_i, g0 : g0 + QUANT_GROUPS, :].rearrange("p g r -> p (g r)"),
-                            in_=grouped[:].rearrange("p g r t -> p (g r t)"),
-                        )
-
-        nc.vector.tensor_scalar_mul(out=turned[:, :, 0:HALF], in0=gain[:, :, HALF:D], scalar1=-1.0)
-        nc.vector.tensor_copy(out=turned[:, :, HALF:D], in_=gain[:, :, 0:HALF])
-        for tab, angle, weight in ((direct_tab, cos_sb, gain), (crossed_tab, sin_sb, turned)):
-            nc.vector.tensor_tensor(
-                out=tab[:, 0:TOKEN_TILES, :],
-                in0=angle[:],
-                in1=weight[:, 0, :].unsqueeze(1).to_broadcast([P, TOKEN_TILES, D]),
-                op=MULT,
-            )
-            nc.vector.tensor_tensor(
-                out=tab[:, TOKEN_TILES, :], in0=angle[:, NEW_TOKENS, :], in1=weight[:, 1, :], op=MULT
-            )
+                        for args in waiting:
+                            quantise(*args)
+                        waiting = [(grouped, tile_i, chunk * X_CHUNK_GROUPS + part * QUANT_GROUPS)]
+            for args in waiting:
+                quantise(*args)
 
         with tc.tile_pool(name="wide", bufs=12) as wide, tc.tile_pool(name="after", bufs=3) as after, tc.psum_pool(name="sums", bufs=8) as sums:
 
@@ -182,8 +177,6 @@ def tile_dflashattention_pa_k_kernel(
                     )
                 rms = after.tile([P, HEADS_PER_BANK], F32, name="rms")
                 nc.scalar.activation(out=rms[:], in_=sum_sq[:], func=ACT.Sqrt, scale=1.0 / D, bias=EPS)
-                rstd = after.tile([P, HEADS_PER_BANK], F32, name="rstd")
-                nc.vector.reciprocal(out=rstd[:], in_=rms[:])
                 res = after.tile(shape, F32, name="res")
                 nc.vector.tensor_tensor(
                     out=res[:], in0=u[:], in1=direct_tab[:, table, :].unsqueeze(1).to_broadcast(shape), op=MULT
@@ -202,6 +195,8 @@ def tile_dflashattention_pa_k_kernel(
                     op=MULT,
                 )
                 nc.vector.tensor_tensor(out=res[:], in0=res[:], in1=crossed[:], op=ADD)
+                rstd = after.tile([P, HEADS_PER_BANK], F32, name="rstd")
+                nc.vector.reciprocal(out=rstd[:], in_=rms[:])
                 nc.vector.tensor_tensor(
                     out=res[:], in0=res[:], in1=rstd[:].unsqueeze(2).to_broadcast(shape), op=MULT
                 )
@@ -240,6 +235,18 @@ def tile_dflashattention_pa_k_kernel(
                 v_sb = after.tile([P, KV_HEADS, D], F32, name="v_sb")
                 nc.vector.tensor_copy(out=v_sb[:].rearrange("p h d -> p (h d)"), in_=v_acc[tile_i][:])
                 store_kv(out_v, tile_i, v_sb)
+            nc.vector.tensor_scalar_mul(out=turned[:, :, 0:HALF], in0=gain[:, :, HALF:D], scalar1=-1.0)
+            nc.vector.tensor_copy(out=turned[:, :, HALF:D], in_=gain[:, :, 0:HALF])
+            for tab, angle, weight in ((direct_tab, cos_sb, gain), (crossed_tab, sin_sb, turned)):
+                nc.vector.tensor_tensor(
+                    out=tab[:, 0:TOKEN_TILES, :],
+                    in0=angle[:],
+                    in1=weight[:, 0, :].unsqueeze(1).to_broadcast([P, TOKEN_TILES, D]),
+                    op=MULT,
+                )
+                nc.vector.tensor_tensor(
+                    out=tab[:, TOKEN_TILES, :], in0=angle[:, NEW_TOKENS, :], in1=weight[:, 1, :], op=MULT
+                )
             for tile_i in range(TOKEN_TILES):
                 store_kv(out_k, tile_i, norm_and_rotate(k_acc[tile_i], tile_i))
 
@@ -256,14 +263,12 @@ def tile_dflashattention_pa_k_kernel(
                     project(q_acc[j], NEW_TOKENS, g, words[:, columns], q_plane(g, columns))
             for a in range(GROUPS // SHARE):
                 words = narrow.tile([P, SHARE, N_PASS], U32, name="words", tag="narrow", align_bytes=64)
-                nc.sync.dma_start(
-                    out=words[:].bitcast(I32),
-                    in_=Wq_words[SHARE * a : SHARE * (a + 1), :, Q_WIDE : HEADS * D, :]
-                    .rearrange("g p n t -> p g (n t)")
-                    .bitcast(I32),
-                )
                 for i in range(SHARE):
                     g = SHARE * a + i
+                    nc.sync.dma_start(
+                        out=words[:, i, :].bitcast(I32),
+                        in_=Wq_words[g, :, Q_WIDE : HEADS * D, :].rearrange("p n t -> p (n t)").bitcast(I32),
+                    )
                     project(q_acc[wide_banks], NEW_TOKENS, g, words[:, i, :], q_plane(g, slice(Q_WIDE, HEADS * D)))
             for j in range(wide_banks + 1):
                 res = norm_and_rotate(q_acc[j], TOKEN_TILES)

@@ -63,18 +63,20 @@ def tile_dflashattention_pa_k_kernel(
     with tc.tile_pool(name="keep", bufs=1) as keep, tc.tile_pool(name="narrow", bufs=8) as narrow, tc.manual_schedule():
         ident = keep.tile([P, P], F32)
         make_identity(nc, ident[:])
+        ones = keep.tile([P, P], BF16)
+        nc.vector.memset(ones[:], 1.0)
+        gain_row = keep.tile([P, 2, D], BF16)
+        nc.vector.memset(gain_row[:], 0.0)
+        gain = keep.tile([P, 2, D], F32)
 
         kv_planes = zeroed_bytes(nc, keep, [P, GROUPS, N_PASS], "kv_planes")
         q_planes = zeroed_bytes(nc, keep, [P, GROUPS // SHARE, HEADS * D], "q_planes")
 
-        small_loads = []
         for r in range(4):
             for offset, scales in ((K_OFFSET, Wk_scales), (V_OFFSET, Wv_scales)):
-                small_loads.append(
-                    (
-                        kv_planes[offset + r : P : 32, :, :].bitcast(I32),
-                        scales[:, r : 16 : 4, :].rearrange("g q n -> q g n").bitcast(I32),
-                    )
+                nc.gpsimd.dma_start(
+                    out=kv_planes[offset + r : P : 32, :, :].bitcast(F32),
+                    in_=scales[:, r : 16 : 4, :].rearrange("g q n -> q g n").bitcast(F32),
                 )
         for a in range(GROUPS // SHARE):
             for quadrant in range(4):
@@ -89,13 +91,13 @@ def tile_dflashattention_pa_k_kernel(
 
         cos_sb = keep.tile([P, TOKEN_TILES, D], BF16)
         sin_sb = keep.tile([P, TOKEN_TILES, D], BF16)
-        gain = keep.tile([P, 2, D], BF16)
+        small_loads = []
         for table, table_sb in ((cos, cos_sb), (sin, sin_sb)):
             small_loads.append((table_sb[:, 0:BATCH, :], table[:, 0:CTX, :].rearrange("b t d -> t b d")))
             for b in range(BATCH):
                 small_loads.append((table_sb[Q_LEN * b : Q_LEN * (b + 1), NEW_TOKENS, :], table[b, CTX:T, :]))
-        small_loads.append((gain[:, 0, :], k_norm_w.partition_broadcast(P)))
-        small_loads.append((gain[:, 1, :], q_norm_w.partition_broadcast(P)))
+        small_loads.append((gain_row[0:1, 0, :], k_norm_w.unsqueeze(0)))
+        small_loads.append((gain_row[0:1, 1, :], q_norm_w.unsqueeze(0)))
 
         x_codes = keep.tile([P, TOKEN_TILES, GROUPS, P], U32, align_bytes=64)
         x_scales = keep.tile([P, TOKEN_TILES, GROUPS, P], U8, align_bytes=64)
@@ -147,6 +149,15 @@ def tile_dflashattention_pa_k_kernel(
                         waiting = [(grouped, tile_i, chunk * X_CHUNK_GROUPS + part * QUANT_GROUPS)]
             for args in waiting:
                 quantise(*args)
+            spread = flip.tile([P, BANK_GROUPS, 2, P], F32, name="flipped")
+            nc.tensor.matmul(
+                out=spread[:, 0, :, :].rearrange("p w d -> p (w d)"),
+                lhsT=ones[:],
+                rhs=gain_row[:].rearrange("p w d -> p (w d)"),
+                start=True,
+                stop=True,
+            )
+            nc.scalar.copy(out=gain[:], in_=spread[:, 0, :, :])
 
         with tc.tile_pool(name="wide", bufs=12) as wide, tc.tile_pool(name="after", bufs=3) as after, tc.psum_pool(name="sums", bufs=8) as sums:
 

@@ -28,6 +28,7 @@ X_CHUNK_GROUPS = 8
 QUANT_GROUPS = 4
 SMALL_PER_BIG = 3
 BANK_GROUPS = 2
+RESULTS = 2 * TOKEN_TILES + HEADS // HEADS_PER_BANK
 Q_WIDE = 3 * N_PASS
 
 FLOPS = 2 * HID * (BATCH * Q_LEN * HEADS * D + 2 * BATCH * T * KV_HEADS * D)
@@ -58,7 +59,11 @@ def tile_dflashattention_pa_k_kernel(
     out_v,
 ):
     nc = tc.nc
-    x_tiles = [target_hidden[0], target_hidden[1], hidden_states.rearrange("b t k -> (b t) k")]
+
+    def x_columns(tile_i, columns):
+        if tile_i == NEW_TOKENS:
+            return hidden_states[:, :, columns].rearrange("b t k -> t b k")
+        return target_hidden[tile_i, :, columns]
 
     with tc.tile_pool(name="keep", bufs=1) as keep, tc.tile_pool(name="narrow", bufs=8) as narrow, tc.manual_schedule():
         ident = keep.tile([P, P], F32)
@@ -94,8 +99,7 @@ def tile_dflashattention_pa_k_kernel(
         small_loads = []
         for table, table_sb in ((cos, cos_sb), (sin, sin_sb)):
             small_loads.append((table_sb[:, 0:BATCH, :], table[:, 0:CTX, :].rearrange("b t d -> t b d")))
-            for b in range(BATCH):
-                small_loads.append((table_sb[Q_LEN * b : Q_LEN * (b + 1), NEW_TOKENS, :], table[b, CTX:T, :]))
+            small_loads.append((table_sb[:, NEW_TOKENS, :], table[:, CTX:T, :].rearrange("b t d -> t b d")))
         small_loads.append((gain_row[0:1, 0, :], k_norm_w.unsqueeze(0)))
         small_loads.append((gain_row[0:1, 1, :], q_norm_w.unsqueeze(0)))
 
@@ -107,7 +111,7 @@ def tile_dflashattention_pa_k_kernel(
                 for tile_i in range(TOKEN_TILES):
                     raw = x_raw.tile([P, X_CHUNK_GROUPS * K_PASS], BF16, name="raw")
                     k0 = chunk * X_CHUNK_GROUPS * K_PASS
-                    nc.sync.dma_start(out=raw[:], in_=x_tiles[tile_i][:, k0 : k0 + X_CHUNK_GROUPS * K_PASS])
+                    nc.sync.dma_start(out=raw[:], in_=x_columns(tile_i, slice(k0, k0 + X_CHUNK_GROUPS * K_PASS)))
                     for sbuf_side, hbm_side in small_loads[SMALL_PER_BIG * len(raws) : SMALL_PER_BIG * (len(raws) + 1)]:
                         nc.sync.dma_start(out=sbuf_side, in_=hbm_side)
                     raws.append(raw)
@@ -159,7 +163,7 @@ def tile_dflashattention_pa_k_kernel(
             )
             nc.scalar.copy(out=gain[:], in_=spread[:, 0, :, :])
 
-        with tc.tile_pool(name="wide", bufs=12) as wide, tc.tile_pool(name="after", bufs=3) as after, tc.psum_pool(name="sums", bufs=8) as sums:
+        with tc.tile_pool(name="wide", bufs=12) as wide, tc.tile_pool(name="after", bufs=2) as after, tc.tile_pool(name="results", bufs=RESULTS) as results, tc.psum_pool(name="sums", bufs=8) as sums:
 
             def project(acc, tile_i, g, words, plane):
                 nc.tensor.matmul_mx(
@@ -188,7 +192,7 @@ def tile_dflashattention_pa_k_kernel(
                     )
                 rms = after.tile([P, HEADS_PER_BANK], F32, name="rms")
                 nc.scalar.activation(out=rms[:], in_=sum_sq[:], func=ACT.Sqrt, scale=1.0 / D, bias=EPS)
-                res = after.tile(shape, F32, name="res")
+                res = results.tile(shape, F32, name="res")
                 nc.vector.tensor_tensor(
                     out=res[:], in0=u[:], in1=direct_tab[:, table, :].unsqueeze(1).to_broadcast(shape), op=MULT
                 )
@@ -213,18 +217,18 @@ def tile_dflashattention_pa_k_kernel(
                 )
                 return res
 
-            def store_new_tokens(queue, out, heads, first_token, res):
+            def store_new_tokens(out, heads, first_token, res):
                 for b in range(BATCH):
-                    queue.dma_start(
+                    nc.sync.dma_start(
                         out=out[b, heads, first_token : first_token + Q_LEN, :].rearrange("h t d -> t h d"),
-                        in_=res[Q_LEN * b : Q_LEN * (b + 1), :, :],
+                        in_=res[b:P:BATCH, :, :],
                     )
 
             def store_kv(out, tile_i, res):
                 if tile_i == NEW_TOKENS:
-                    store_new_tokens(nc.gpsimd, out, slice(0, KV_HEADS), CTX, res)
+                    store_new_tokens(out, slice(0, KV_HEADS), CTX, res)
                 else:
-                    nc.gpsimd.dma_start(out=out[tile_i, :, 0:CTX, :].rearrange("h t d -> t h d"), in_=res[:])
+                    nc.sync.dma_start(out=out[tile_i, :, 0:CTX, :].rearrange("h t d -> t h d"), in_=res[:])
 
             v_acc = [sums.tile([P, N_PASS], F32, name="v_acc%d" % i, tag="acc") for i in range(TOKEN_TILES)]
             k_acc = [sums.tile([P, N_PASS], F32, name="k_acc%d" % i, tag="acc") for i in range(TOKEN_TILES)]
@@ -242,10 +246,11 @@ def tile_dflashattention_pa_k_kernel(
                     for tile_i in range(TOKEN_TILES):
                         project(v_acc[tile_i], tile_i, g, loaded[0][:, i, :], kv_planes[V_OFFSET:P, g, :])
                         project(k_acc[tile_i], tile_i, g, loaded[1][:, i, :], kv_planes[K_OFFSET:P, g, :])
+            v_res = []
             for tile_i in range(TOKEN_TILES):
-                v_sb = after.tile([P, KV_HEADS, D], F32, name="v_sb")
+                v_sb = results.tile([P, KV_HEADS, D], F32, name="res")
                 nc.vector.tensor_copy(out=v_sb[:].rearrange("p h d -> p (h d)"), in_=v_acc[tile_i][:])
-                store_kv(out_v, tile_i, v_sb)
+                v_res.append(v_sb)
             nc.vector.tensor_scalar_mul(out=turned[:, :, 0:HALF], in0=gain[:, :, HALF:D], scalar1=-1.0)
             nc.vector.tensor_copy(out=turned[:, :, HALF:D], in_=gain[:, :, 0:HALF])
             for tab, angle, weight in ((direct_tab, cos_sb, gain), (crossed_tab, sin_sb, turned)):
@@ -258,8 +263,7 @@ def tile_dflashattention_pa_k_kernel(
                 nc.vector.tensor_tensor(
                     out=tab[:, TOKEN_TILES, :], in0=angle[:, NEW_TOKENS, :], in1=weight[:, 1, :], op=MULT
                 )
-            for tile_i in range(TOKEN_TILES):
-                store_kv(out_k, tile_i, norm_and_rotate(k_acc[tile_i], tile_i))
+            k_res = [norm_and_rotate(k_acc[tile_i], tile_i) for tile_i in range(TOKEN_TILES)]
 
             wide_banks = Q_WIDE // N_PASS
             q_acc = [sums.tile([P, N_PASS], F32, name="q_acc%d" % j, tag="acc") for j in range(wide_banks + 1)]
@@ -281,6 +285,9 @@ def tile_dflashattention_pa_k_kernel(
                         in_=Wq_words[g, :, Q_WIDE : HEADS * D, :].rearrange("p n t -> p (n t)").bitcast(I32),
                     )
                     project(q_acc[wide_banks], NEW_TOKENS, g, words[:, i, :], q_plane(g, slice(Q_WIDE, HEADS * D)))
+            for tile_i in range(TOKEN_TILES):
+                store_kv(out_v, tile_i, v_res[tile_i])
+                store_kv(out_k, tile_i, k_res[tile_i])
             for j in range(wide_banks + 1):
                 res = norm_and_rotate(q_acc[j], TOKEN_TILES)
-                store_new_tokens(nc.sync, out_q, slice(HEADS_PER_BANK * j, HEADS_PER_BANK * (j + 1)), 0, res)
+                store_new_tokens(out_q, slice(HEADS_PER_BANK * j, HEADS_PER_BANK * (j + 1)), 0, res)

@@ -23,7 +23,8 @@ HEADS_PER_BANK = N_PASS // D
 TOKEN_TILES = 3
 NEW_TOKENS = 2
 SHARE = 4
-K_OFFSET, V_OFFSET = 0, 4
+K_OFFSET, V_OFFSET = 0, 8
+KV_SHARE = 2
 X_CHUNK_GROUPS = 8
 QUANT_GROUPS = 4
 SMALL_PER_BIG = 3
@@ -74,15 +75,16 @@ def tile_dflashattention_pa_k_kernel(
         nc.vector.memset(gain_row[:], 0.0)
         gain = keep.tile([P, 2, D], F32)
 
-        kv_planes = zeroed_bytes(nc, keep, [P, GROUPS, N_PASS], "kv_planes")
+        kv_planes = zeroed_bytes(nc, keep, [P, GROUPS // KV_SHARE, N_PASS], "kv_planes")
         q_planes = zeroed_bytes(nc, keep, [P, GROUPS // SHARE, HEADS * D], "q_planes")
 
         for r in range(4):
-            for offset, scales in ((K_OFFSET, Wk_scales), (V_OFFSET, Wv_scales)):
-                nc.gpsimd.dma_start(
-                    out=kv_planes[offset + r : P : 32, :, :].bitcast(F32),
-                    in_=scales[:, r : 16 : 4, :].rearrange("g q n -> q g n").bitcast(F32),
-                )
+            for i in range(KV_SHARE):
+                for offset, scales in ((K_OFFSET, Wk_scales), (V_OFFSET, Wv_scales)):
+                    nc.gpsimd.dma_start(
+                        out=kv_planes[offset + 4 * i + r : P : 32, :, :].bitcast(F32),
+                        in_=scales[i : GROUPS : KV_SHARE, r : 16 : 4, :].rearrange("g q n -> q g n").bitcast(F32),
+                    )
         for a in range(GROUPS // SHARE):
             for quadrant in range(4):
                 nc.gpsimd.dma_start(
@@ -179,6 +181,9 @@ def tile_dflashattention_pa_k_kernel(
             def q_plane(g, columns):
                 return q_planes[4 * (g % SHARE) : P, g // SHARE, columns]
 
+            def kv_plane(offset, g):
+                return kv_planes[offset + 4 * (g % KV_SHARE) : P, g // KV_SHARE, :]
+
             def norm_and_rotate(acc, table):
                 shape = [P, HEADS_PER_BANK, D]
                 half_shape = [P, HEADS_PER_BANK, HALF]
@@ -244,8 +249,8 @@ def tile_dflashattention_pa_k_kernel(
                 for i in range(SHARE):
                     g = SHARE * a + i
                     for tile_i in range(TOKEN_TILES):
-                        project(v_acc[tile_i], tile_i, g, loaded[0][:, i, :], kv_planes[V_OFFSET:P, g, :])
-                        project(k_acc[tile_i], tile_i, g, loaded[1][:, i, :], kv_planes[K_OFFSET:P, g, :])
+                        project(v_acc[tile_i], tile_i, g, loaded[0][:, i, :], kv_plane(V_OFFSET, g))
+                        project(k_acc[tile_i], tile_i, g, loaded[1][:, i, :], kv_plane(K_OFFSET, g))
             v_res = []
             for tile_i in range(TOKEN_TILES):
                 v_sb = results.tile([P, KV_HEADS, D], F32, name="res")

@@ -21,6 +21,7 @@ GROUPS = HID // K_PASS
 N_PASS = 512
 HEADS_PER_BANK = N_PASS // D
 TOKEN_TILES = 3
+CTX_TILES = 2
 NEW_TOKENS = 2
 SHARE = 4
 K_OFFSET, V_OFFSET = 0, 8
@@ -29,7 +30,6 @@ X_CHUNK_GROUPS = 8
 QUANT_GROUPS = 4
 SMALL_PER_BIG = 3
 BANK_GROUPS = 2
-RESULTS = 2 * TOKEN_TILES + HEADS // HEADS_PER_BANK
 Q_WIDE = 3 * N_PASS
 
 FLOPS = 2 * HID * (BATCH * Q_LEN * HEADS * D + 2 * BATCH * T * KV_HEADS * D)
@@ -64,7 +64,7 @@ def tile_dflashattention_pa_k_kernel(
     def x_columns(tile_i, columns):
         if tile_i == NEW_TOKENS:
             return hidden_states[:, :, columns].rearrange("b t k -> t b k")
-        return target_hidden[tile_i, :, columns]
+        return target_hidden[:, tile_i:CTX:CTX_TILES, columns].rearrange("b t k -> t b k")
 
     with tc.tile_pool(name="keep", bufs=1) as keep, tc.tile_pool(name="narrow", bufs=8) as narrow, tc.manual_schedule():
         ident = keep.tile([P, P], F32)
@@ -100,7 +100,9 @@ def tile_dflashattention_pa_k_kernel(
         sin_sb = keep.tile([P, TOKEN_TILES, D], BF16)
         small_loads = []
         for table, table_sb in ((cos, cos_sb), (sin, sin_sb)):
-            small_loads.append((table_sb[:, 0:BATCH, :], table[:, 0:CTX, :].rearrange("b t d -> t b d")))
+            small_loads.append(
+                (table_sb[:, 0:CTX_TILES, :], table[:, 0:CTX, :].rearrange("b (j i) d -> j b (i d)", i=CTX_TILES))
+            )
             small_loads.append((table_sb[:, NEW_TOKENS, :], table[:, CTX:T, :].rearrange("b t d -> t b d")))
         small_loads.append((gain_row[0:1, 0, :], k_norm_w.unsqueeze(0)))
         small_loads.append((gain_row[0:1, 1, :], q_norm_w.unsqueeze(0)))
@@ -165,7 +167,7 @@ def tile_dflashattention_pa_k_kernel(
             )
             nc.scalar.copy(out=gain[:], in_=spread[:, 0, :, :])
 
-        with tc.tile_pool(name="wide", bufs=12) as wide, tc.tile_pool(name="after", bufs=2) as after, tc.tile_pool(name="results", bufs=RESULTS) as results, tc.psum_pool(name="sums", bufs=8) as sums:
+        with tc.tile_pool(name="wide", bufs=12) as wide, tc.tile_pool(name="after", bufs=2) as after, tc.tile_pool(name="results", bufs=1) as results, tc.psum_pool(name="sums", bufs=8) as sums:
 
             def project(acc, tile_i, g, words, plane):
                 nc.tensor.matmul_mx(
@@ -184,7 +186,7 @@ def tile_dflashattention_pa_k_kernel(
             def kv_plane(offset, g):
                 return kv_planes[offset + 4 * (g % KV_SHARE) : P, g // KV_SHARE, :]
 
-            def norm_and_rotate(acc, table):
+            def norm_and_rotate(acc, table, res):
                 shape = [P, HEADS_PER_BANK, D]
                 half_shape = [P, HEADS_PER_BANK, HALF]
                 u = after.tile(shape, F32, name="u")
@@ -197,9 +199,8 @@ def tile_dflashattention_pa_k_kernel(
                     )
                 rms = after.tile([P, HEADS_PER_BANK], F32, name="rms")
                 nc.scalar.activation(out=rms[:], in_=sum_sq[:], func=ACT.Sqrt, scale=1.0 / D, bias=EPS)
-                res = results.tile(shape, F32, name="res")
                 nc.vector.tensor_tensor(
-                    out=res[:], in0=u[:], in1=direct_tab[:, table, :].unsqueeze(1).to_broadcast(shape), op=MULT
+                    out=res, in0=u[:], in1=direct_tab[:, table, :].unsqueeze(1).to_broadcast(shape), op=MULT
                 )
                 crossed = after.tile(shape, F32, name="crossed")
                 nc.vector.tensor_tensor(
@@ -214,13 +215,10 @@ def tile_dflashattention_pa_k_kernel(
                     in1=crossed_tab[:, table, HALF:D].unsqueeze(1).to_broadcast(half_shape),
                     op=MULT,
                 )
-                nc.vector.tensor_tensor(out=res[:], in0=res[:], in1=crossed[:], op=ADD)
+                nc.vector.tensor_tensor(out=res, in0=res, in1=crossed[:], op=ADD)
                 rstd = after.tile([P, HEADS_PER_BANK], F32, name="rstd")
                 nc.vector.reciprocal(out=rstd[:], in_=rms[:])
-                nc.vector.tensor_tensor(
-                    out=res[:], in0=res[:], in1=rstd[:].unsqueeze(2).to_broadcast(shape), op=MULT
-                )
-                return res
+                nc.vector.tensor_tensor(out=res, in0=res, in1=rstd[:].unsqueeze(2).to_broadcast(shape), op=MULT)
 
             def store_new_tokens(out, heads, first_token, res):
                 for b in range(BATCH):
@@ -229,11 +227,12 @@ def tile_dflashattention_pa_k_kernel(
                         in_=res[b:P:BATCH, :, :],
                     )
 
-            def store_kv(out, tile_i, res):
-                if tile_i == NEW_TOKENS:
-                    store_new_tokens(out, slice(0, KV_HEADS), CTX, res)
-                else:
-                    nc.sync.dma_start(out=out[tile_i, :, 0:CTX, :].rearrange("h t d -> t h d"), in_=res[:])
+            def store_context(out, res):
+                for b in range(BATCH):
+                    nc.sync.dma_start(
+                        out=out[b, :, 0:CTX, :].rearrange("h (j i) d -> j h (i d)", i=CTX_TILES),
+                        in_=res[b:P:BATCH, :, :, :].rearrange("p h i d -> p h (i d)"),
+                    )
 
             v_acc = [sums.tile([P, N_PASS], F32, name="v_acc%d" % i, tag="acc") for i in range(TOKEN_TILES)]
             k_acc = [sums.tile([P, N_PASS], F32, name="k_acc%d" % i, tag="acc") for i in range(TOKEN_TILES)]
@@ -251,11 +250,14 @@ def tile_dflashattention_pa_k_kernel(
                     for tile_i in range(TOKEN_TILES):
                         project(v_acc[tile_i], tile_i, g, loaded[0][:, i, :], kv_plane(V_OFFSET, g))
                         project(k_acc[tile_i], tile_i, g, loaded[1][:, i, :], kv_plane(K_OFFSET, g))
-            v_res = []
+            v_context = results.tile([P, KV_HEADS, CTX_TILES, D], F32)
+            k_context = results.tile([P, KV_HEADS, CTX_TILES, D], F32)
+            v_new = results.tile([P, KV_HEADS, D], F32)
+            k_new = results.tile([P, KV_HEADS, D], F32)
+            v_res = [v_context[:, :, i, :] for i in range(CTX_TILES)] + [v_new[:]]
+            k_res = [k_context[:, :, i, :] for i in range(CTX_TILES)] + [k_new[:]]
             for tile_i in range(TOKEN_TILES):
-                v_sb = results.tile([P, KV_HEADS, D], F32, name="res")
-                nc.vector.tensor_copy(out=v_sb[:].rearrange("p h d -> p (h d)"), in_=v_acc[tile_i][:])
-                v_res.append(v_sb)
+                nc.vector.tensor_copy(out=v_res[tile_i], in_=v_acc[tile_i][:].rearrange("p (h d) -> p h d", d=D))
             nc.vector.tensor_scalar_mul(out=turned[:, :, 0:HALF], in0=gain[:, :, HALF:D], scalar1=-1.0)
             nc.vector.tensor_copy(out=turned[:, :, HALF:D], in_=gain[:, :, 0:HALF])
             for tab, angle, weight in ((direct_tab, cos_sb, gain), (crossed_tab, sin_sb, turned)):
@@ -268,7 +270,8 @@ def tile_dflashattention_pa_k_kernel(
                 nc.vector.tensor_tensor(
                     out=tab[:, TOKEN_TILES, :], in0=angle[:, NEW_TOKENS, :], in1=weight[:, 1, :], op=MULT
                 )
-            k_res = [norm_and_rotate(k_acc[tile_i], tile_i) for tile_i in range(TOKEN_TILES)]
+            for tile_i in range(TOKEN_TILES):
+                norm_and_rotate(k_acc[tile_i], tile_i, k_res[tile_i])
 
             wide_banks = Q_WIDE // N_PASS
             q_acc = [sums.tile([P, N_PASS], F32, name="q_acc%d" % j, tag="acc") for j in range(wide_banks + 1)]
@@ -290,9 +293,10 @@ def tile_dflashattention_pa_k_kernel(
                         in_=Wq_words[g, :, Q_WIDE : HEADS * D, :].rearrange("p n t -> p (n t)").bitcast(I32),
                     )
                     project(q_acc[wide_banks], NEW_TOKENS, g, words[:, i, :], q_plane(g, slice(Q_WIDE, HEADS * D)))
-            for tile_i in range(TOKEN_TILES):
-                store_kv(out_v, tile_i, v_res[tile_i])
-                store_kv(out_k, tile_i, k_res[tile_i])
+            for out, context, new in ((out_v, v_context, v_new), (out_k, k_context, k_new)):
+                store_context(out, context)
+                store_new_tokens(out, slice(0, KV_HEADS), CTX, new)
             for j in range(wide_banks + 1):
-                res = norm_and_rotate(q_acc[j], TOKEN_TILES)
+                res = results.tile([P, HEADS_PER_BANK, D], F32, name="q_res%d" % j)
+                norm_and_rotate(q_acc[j], TOKEN_TILES, res[:])
                 store_new_tokens(out_q, slice(HEADS_PER_BANK * j, HEADS_PER_BANK * (j + 1)), 0, res)

@@ -167,7 +167,7 @@ def tile_dflashattention_pa_k_kernel(
             )
             nc.scalar.copy(out=gain[:], in_=spread[:, 0, :, :])
 
-        with tc.tile_pool(name="wide", bufs=12) as wide, tc.tile_pool(name="after", bufs=2) as after, tc.tile_pool(name="results", bufs=1) as results, tc.psum_pool(name="sums", bufs=8) as sums:
+        with tc.tile_pool(name="wide", bufs=14) as wide, tc.tile_pool(name="after", bufs=2) as after, tc.tile_pool(name="results", bufs=1) as results, tc.psum_pool(name="sums", bufs=8) as sums:
 
             def project(acc, tile_i, g, words, plane):
                 nc.tensor.matmul_mx(

@@ -240,11 +240,13 @@ def tile_dflashattention_pa_k_kernel(
                 loaded = []
                 for words_in in (Wv_words, Wk_words):
                     words = narrow.tile([P, SHARE, N_PASS], U32, name="words", tag="narrow", align_bytes=64)
-                    nc.sync.dma_start(
-                        out=words[:].bitcast(I32),
-                        in_=words_in[SHARE * a : SHARE * (a + 1)].rearrange("g p n t -> p g (n t)").bitcast(I32),
-                    )
                     loaded.append(words)
+                for i in range(SHARE):
+                    for words, words_in in zip(loaded, (Wv_words, Wk_words)):
+                        nc.sync.dma_start(
+                            out=words[:, i, :].bitcast(I32),
+                            in_=words_in[SHARE * a + i].rearrange("p n t -> p (n t)").bitcast(I32),
+                        )
                 for i in range(SHARE):
                     g = SHARE * a + i
                     for tile_i in range(TOKEN_TILES):

@@ -28,7 +28,6 @@ K_OFFSET, V_OFFSET = 0, 8
 KV_SHARE = 2
 X_CHUNK_GROUPS = 8
 QUANT_GROUPS = 4
-SMALL_PER_BIG = 3
 BANK_GROUPS = 2
 Q_WIDE = 3 * N_PASS
 
@@ -98,14 +97,12 @@ def tile_dflashattention_pa_k_kernel(
 
         cos_sb = keep.tile([P, TOKEN_TILES, D], BF16)
         sin_sb = keep.tile([P, TOKEN_TILES, D], BF16)
-        small_loads = []
         for table, table_sb in ((cos, cos_sb), (sin, sin_sb)):
-            small_loads.append(
-                (table_sb[:, 0:CTX_TILES, :], table[:, 0:CTX, :].rearrange("b (j i) d -> j b (i d)", i=CTX_TILES))
+            nc.gpsimd.dma_start(
+                out=table_sb[:, 0:CTX_TILES, :],
+                in_=table[:, 0:CTX, :].rearrange("b (j i) d -> j b (i d)", i=CTX_TILES),
             )
-            small_loads.append((table_sb[:, NEW_TOKENS, :], table[:, CTX:T, :].rearrange("b t d -> t b d")))
-        small_loads.append((gain_row[0:1, 0, :], k_norm_w.unsqueeze(0)))
-        small_loads.append((gain_row[0:1, 1, :], q_norm_w.unsqueeze(0)))
+            nc.gpsimd.dma_start(out=table_sb[:, NEW_TOKENS, :], in_=table[:, CTX:T, :].rearrange("b t d -> t b d"))
 
         x_codes = keep.tile([P, TOKEN_TILES, GROUPS, P], U32, align_bytes=64)
         x_scales = keep.tile([P, TOKEN_TILES, GROUPS, P], U8, align_bytes=64)
@@ -116,10 +113,9 @@ def tile_dflashattention_pa_k_kernel(
                     raw = x_raw.tile([P, X_CHUNK_GROUPS * K_PASS], BF16, name="raw")
                     k0 = chunk * X_CHUNK_GROUPS * K_PASS
                     nc.sync.dma_start(out=raw[:], in_=x_columns(tile_i, slice(k0, k0 + X_CHUNK_GROUPS * K_PASS)))
-                    for sbuf_side, hbm_side in small_loads[SMALL_PER_BIG * len(raws) : SMALL_PER_BIG * (len(raws) + 1)]:
-                        nc.sync.dma_start(out=sbuf_side, in_=hbm_side)
                     raws.append(raw)
-            assert SMALL_PER_BIG * len(raws) >= len(small_loads)
+            nc.sync.dma_start(out=gain_row[0:1, 0, :], in_=k_norm_w.unsqueeze(0))
+            nc.sync.dma_start(out=gain_row[0:1, 1, :], in_=q_norm_w.unsqueeze(0))
 
             def quantise(grouped, tile_i, g0):
                 nc.vector.quantize_mx(

@@ -294,7 +294,11 @@ def tile_dflashattention_pa_k_kernel(
             for out, context, new in ((out_v, v_context, v_new), (out_k, k_context, k_new)):
                 store_context(out, context)
                 store_new_tokens(out, slice(0, KV_HEADS), CTX, new)
-            for j in range(wide_banks + 1):
-                res = results.tile([P, HEADS_PER_BANK, D], F32, name="q_res%d" % j)
-                norm_and_rotate(q_acc[j], TOKEN_TILES, res[:])
-                store_new_tokens(out_q, slice(HEADS_PER_BANK * j, HEADS_PER_BANK * (j + 1)), 0, res)
+            wide_heads = HEADS_PER_BANK * wide_banks
+            q_wide = results.tile([P, wide_heads, D], F32)
+            q_last = results.tile([P, HEADS_PER_BANK, D], F32)
+            for j in range(wide_banks):
+                norm_and_rotate(q_acc[j], TOKEN_TILES, q_wide[:, HEADS_PER_BANK * j : HEADS_PER_BANK * (j + 1), :])
+            store_new_tokens(out_q, slice(0, wide_heads), 0, q_wide)
+            norm_and_rotate(q_acc[wide_banks], TOKEN_TILES, q_last[:])
+            store_new_tokens(out_q, slice(wide_heads, HEADS), 0, q_last)

import concourse.mybir as mybir
from concourse.masks import make_identity

F32 = mybir.dt.float32
BF16 = mybir.dt.bfloat16
I32 = mybir.dt.int32
U32 = mybir.dt.uint32
U8 = mybir.dt.uint8
FP8X4 = mybir.dt.float8_e4m3fn_x4
MULT = mybir.AluOpType.mult
ADD = mybir.AluOpType.add
ACT = mybir.ActivationFunctionType

P = 128
BATCH, Q_LEN, CTX, HID, HEADS, KV_HEADS, D = 2, 64, 128, 8192, 16, 4, 128
T = CTX + Q_LEN
HALF = D // 2
EPS = 1e-6
K_PASS = 512
GROUPS = HID // K_PASS
N_PASS = 512
HEADS_PER_BANK = N_PASS // D
TOKEN_TILES = 3
CTX_TILES = 2
NEW_TOKENS = 2
SHARE = 4
K_OFFSET, V_OFFSET = 0, 8
KV_SHARE = 2
X_CHUNK_GROUPS = 8
QUANT_GROUPS = 4
BANK_GROUPS = 2
Q_WIDE = 3 * N_PASS

FLOPS = 2 * HID * (BATCH * Q_LEN * HEADS * D + 2 * BATCH * T * KV_HEADS * D)


def zeroed_bytes(nc, pool, shape, name):
    planes = pool.tile(shape, U8, name=name, align_bytes=64)
    nc.vector.memset(planes[:].rearrange("p a n -> p (a n)").bitcast(I32), 0)
    return planes


def tile_dflashattention_pa_k_kernel(
    tc,
    hidden_states,
    target_hidden,
    cos,
    sin,
    Wq_words,
    Wq_scales,
    Wk_words,
    Wk_scales,
    Wv_words,
    Wv_scales,
    q_norm_w,
    k_norm_w,
    out_q,
    out_k,
    out_v,
):
    nc = tc.nc

    def x_columns(tile_i, columns):
        if tile_i == NEW_TOKENS:
            return hidden_states[:, :, columns].rearrange("b t k -> t b k")
        return target_hidden[:, tile_i:CTX:CTX_TILES, columns].rearrange("b t k -> t b k")

    with tc.tile_pool(name="keep", bufs=1) as keep, tc.tile_pool(name="narrow", bufs=8) as narrow, tc.manual_schedule():
        ident = keep.tile([P, P], F32)
        make_identity(nc, ident[:])
        ones = keep.tile([P, P], BF16)
        nc.vector.memset(ones[:], 1.0)
        gain_row = keep.tile([P, 2, D], BF16)
        nc.vector.memset(gain_row[:], 0.0)
        gain = keep.tile([P, 2, D], F32)

        kv_planes = zeroed_bytes(nc, keep, [P, GROUPS // KV_SHARE, N_PASS], "kv_planes")
        q_planes = zeroed_bytes(nc, keep, [P, GROUPS // SHARE, HEADS * D], "q_planes")

        for r in range(4):
            for i in range(KV_SHARE):
                for offset, scales in ((K_OFFSET, Wk_scales), (V_OFFSET, Wv_scales)):
                    nc.gpsimd.dma_start(
                        out=kv_planes[offset + 4 * i + r : P : 32, :, :].bitcast(F32),
                        in_=scales[i : GROUPS : KV_SHARE, r : 16 : 4, :].rearrange("g q n -> q g n").bitcast(F32),
                    )
        for a in range(GROUPS // SHARE):
            for quadrant in range(4):
                nc.gpsimd.dma_start(
                    out=q_planes[32 * quadrant : 32 * quadrant + 4 * SHARE, a, :].bitcast(F32),
                    in_=Wq_scales[SHARE * a : SHARE * (a + 1), 4 * quadrant : 4 * quadrant + 4, :].bitcast(F32),
                )

        turned = keep.tile([P, 2, D], F32)
        direct_tab = keep.tile([P, TOKEN_TILES + 1, D], F32)
        crossed_tab = keep.tile([P, TOKEN_TILES + 1, D], F32)

        cos_sb = keep.tile([P, TOKEN_TILES, D], BF16)
        sin_sb = keep.tile([P, TOKEN_TILES, D], BF16)
        for table, table_sb in ((cos, cos_sb), (sin, sin_sb)):
            nc.gpsimd.dma_start(
                out=table_sb[:, 0:CTX_TILES, :],
                in_=table[:, 0:CTX, :].rearrange("b (j i) d -> j b (i d)", i=CTX_TILES),
            )
            nc.gpsimd.dma_start(out=table_sb[:, NEW_TOKENS, :], in_=table[:, CTX:T, :].rearrange("b t d -> t b d"))

        x_codes = keep.tile([P, TOKEN_TILES, GROUPS, P], U32, align_bytes=64)
        x_scales = keep.tile([P, TOKEN_TILES, GROUPS, P], U8, align_bytes=64)
        with tc.tile_pool(name="x_raw", bufs=6) as x_raw, tc.tile_pool(name="stage", bufs=4) as stage, tc.psum_pool(name="flip", bufs=8) as flip:
            raws = []
            for chunk in range(GROUPS // X_CHUNK_GROUPS):
                for tile_i in range(TOKEN_TILES):
                    raw = x_raw.tile([P, X_CHUNK_GROUPS * K_PASS], BF16, name="raw")
                    k0 = chunk * X_CHUNK_GROUPS * K_PASS
                    nc.sync.dma_start(out=raw[:], in_=x_columns(tile_i, slice(k0, k0 + X_CHUNK_GROUPS * K_PASS)))
                    raws.append(raw)
            nc.sync.dma_start(out=gain_row[0:1, 0, :], in_=k_norm_w.unsqueeze(0))
            nc.sync.dma_start(out=gain_row[0:1, 1, :], in_=q_norm_w.unsqueeze(0))

            def quantise(grouped, tile_i, g0):
                nc.vector.quantize_mx(
                    out=x_codes[:, tile_i, g0 : g0 + QUANT_GROUPS, :].rearrange("p g r -> p (g r)").bitcast(FP8X4),
                    scales=x_scales[:, tile_i, g0 : g0 + QUANT_GROUPS, :].rearrange("p g r -> p (g r)"),
                    in_=grouped[:].rearrange("p g r t -> p (g r t)"),
                )

            waiting = []
            for chunk in range(GROUPS // X_CHUNK_GROUPS):
                for tile_i in range(TOKEN_TILES):
                    raw = raws[chunk * TOKEN_TILES + tile_i]
                    pairs = raw[:].bitcast(F32)
                    pairs_per_group = K_PASS // 2
                    for part in range(X_CHUNK_GROUPS // QUANT_GROUPS):
                        grouped = stage.tile([P, QUANT_GROUPS, P, 4], BF16, align_bytes=64)
                        for bank in range(QUANT_GROUPS // BANK_GROUPS):
                            flipped = flip.tile([P, BANK_GROUPS, 2, P], F32)
                            for j in range(BANK_GROUPS):
                                first = (part * QUANT_GROUPS + bank * BANK_GROUPS + j) * pairs_per_group
                                for u in range(2):
                                    nc.tensor.transpose(
                                        flipped[:, j, u, :],
                                        pairs[:, first + u : first + pairs_per_group : 2],
                                        ident[:],
                                    )
                            dst = grouped[:, bank * BANK_GROUPS : (bank + 1) * BANK_GROUPS, :, :].bitcast(F32)
                            src = flipped[:].rearrange("p j u r -> p j r u")
                            if (part * (QUANT_GROUPS // BANK_GROUPS) + bank) % 4 == 3:
                                nc.vector.tensor_copy(out=dst, in_=src)
                            else:
                                nc.scalar.copy(out=dst, in_=src)
                        for args in waiting:
                            quantise(*args)
                        waiting = [(grouped, tile_i, chunk * X_CHUNK_GROUPS + part * QUANT_GROUPS)]
            for args in waiting:
                quantise(*args)
            spread = flip.tile([P, BANK_GROUPS, 2, P], F32, name="flipped")
            nc.tensor.matmul(
                out=spread[:, 0, :, :].rearrange("p w d -> p (w d)"),
                lhsT=ones[:],
                rhs=gain_row[:].rearrange("p w d -> p (w d)"),
                start=True,
                stop=True,
            )
            nc.scalar.copy(out=gain[:], in_=spread[:, 0, :, :])

        with tc.tile_pool(name="wide", bufs=14) as wide, tc.tile_pool(name="after", bufs=2) as after, tc.tile_pool(name="results", bufs=1) as results, tc.psum_pool(name="sums", bufs=8) as sums:

            def project(acc, tile_i, g, words, plane):
                nc.tensor.matmul_mx(
                    out=acc[:],
                    lhsT=x_codes[:, tile_i, g, :].bitcast(FP8X4),
                    lhsT_scale=x_scales[:, tile_i, g, :],
                    rhs=words.bitcast(FP8X4),
                    rhs_scale=plane,
                    start=(g == 0),
                    stop=(g == GROUPS - 1),
                )

            def q_plane(g, columns):
                return q_planes[4 * (g % SHARE) : P, g // SHARE, columns]

            def kv_plane(offset, g):
                return kv_planes[offset + 4 * (g % KV_SHARE) : P, g // KV_SHARE, :]

            def norm_and_rotate(acc, table, res):
                shape = [P, HEADS_PER_BANK, D]
                half_shape = [P, HEADS_PER_BANK, HALF]
                u = after.tile(shape, F32, name="u")
                nc.scalar.copy(out=u[:].rearrange("p h d -> p (h d)"), in_=acc[:])
                squares = after.tile(shape, F32, name="squares")
                sum_sq = after.tile([P, HEADS_PER_BANK], F32, name="sum_sq")
                for h in range(HEADS_PER_BANK):
                    nc.scalar.activation(
                        out=squares[:, h, :], in_=u[:, h, :], func=ACT.Square, accum_out=sum_sq[:, h : h + 1]
                    )
                rms = after.tile([P, HEADS_PER_BANK], F32, name="rms")
                nc.scalar.activation(out=rms[:], in_=sum_sq[:], func=ACT.Sqrt, scale=1.0 / D, bias=EPS)
                nc.vector.tensor_tensor(
                    out=res, in0=u[:], in1=direct_tab[:, table, :].unsqueeze(1).to_broadcast(shape), op=MULT
                )
                crossed = after.tile(shape, F32, name="crossed")
                nc.vector.tensor_tensor(
                    out=crossed[:, :, 0:HALF],
                    in0=u[:, :, HALF:D],
                    in1=crossed_tab[:, table, 0:HALF].unsqueeze(1).to_broadcast(half_shape),
                    op=MULT,
                )
                nc.vector.tensor_tensor(
                    out=crossed[:, :, HALF:D],
                    in0=u[:, :, 0:HALF],
                    in1=crossed_tab[:, table, HALF:D].unsqueeze(1).to_broadcast(half_shape),
                    op=MULT,
                )
                nc.vector.tensor_tensor(out=res, in0=res, in1=crossed[:], op=ADD)
                rstd = after.tile([P, HEADS_PER_BANK], F32, name="rstd")
                nc.vector.reciprocal(out=rstd[:], in_=rms[:])
                nc.vector.tensor_tensor(out=res, in0=res, in1=rstd[:].unsqueeze(2).to_broadcast(shape), op=MULT)

            def store_new_tokens(out, heads, first_token, res):
                for b in range(BATCH):
                    nc.sync.dma_start(
                        out=out[b, heads, first_token : first_token + Q_LEN, :].rearrange("h t d -> t h d"),
                        in_=res[b:P:BATCH, :, :],
                    )

            def store_context(out, res):
                for b in range(BATCH):
                    nc.sync.dma_start(
                        out=out[b, :, 0:CTX, :].rearrange("h (j i) d -> j h (i d)", i=CTX_TILES),
                        in_=res[b:P:BATCH, :, :, :].rearrange("p h i d -> p h (i d)"),
                    )

            v_acc = [sums.tile([P, N_PASS], F32, name="v_acc%d" % i, tag="acc") for i in range(TOKEN_TILES)]
            k_acc = [sums.tile([P, N_PASS], F32, name="k_acc%d" % i, tag="acc") for i in range(TOKEN_TILES)]
            for a in range(GROUPS // SHARE):
                loaded = []
                for words_in in (Wv_words, Wk_words):
                    words = narrow.tile([P, SHARE, N_PASS], U32, name="words", tag="narrow", align_bytes=64)
                    loaded.append(words)
                for i in range(SHARE):
                    for words, words_in in zip(loaded, (Wv_words, Wk_words)):
                        nc.sync.dma_start(
                            out=words[:, i, :].bitcast(I32),
                            in_=words_in[SHARE * a + i].rearrange("p n t -> p (n t)").bitcast(I32),
                        )
                for i in range(SHARE):
                    g = SHARE * a + i
                    for tile_i in range(TOKEN_TILES):
                        project(v_acc[tile_i], tile_i, g, loaded[0][:, i, :], kv_plane(V_OFFSET, g))
                        project(k_acc[tile_i], tile_i, g, loaded[1][:, i, :], kv_plane(K_OFFSET, g))
            v_context = results.tile([P, KV_HEADS, CTX_TILES, D], F32)
            k_context = results.tile([P, KV_HEADS, CTX_TILES, D], F32)
            v_new = results.tile([P, KV_HEADS, D], F32)
            k_new = results.tile([P, KV_HEADS, D], F32)
            v_res = [v_context[:, :, i, :] for i in range(CTX_TILES)] + [v_new[:]]
            k_res = [k_context[:, :, i, :] for i in range(CTX_TILES)] + [k_new[:]]
            for tile_i in range(TOKEN_TILES):
                nc.vector.tensor_copy(out=v_res[tile_i], in_=v_acc[tile_i][:].rearrange("p (h d) -> p h d", d=D))
            nc.vector.tensor_scalar_mul(out=turned[:, :, 0:HALF], in0=gain[:, :, HALF:D], scalar1=-1.0)
            nc.vector.tensor_copy(out=turned[:, :, HALF:D], in_=gain[:, :, 0:HALF])
            for tab, angle, weight in ((direct_tab, cos_sb, gain), (crossed_tab, sin_sb, turned)):
                nc.vector.tensor_tensor(
                    out=tab[:, 0:TOKEN_TILES, :],
                    in0=angle[:],
                    in1=weight[:, 0, :].unsqueeze(1).to_broadcast([P, TOKEN_TILES, D]),
                    op=MULT,
                )
                nc.vector.tensor_tensor(
                    out=tab[:, TOKEN_TILES, :], in0=angle[:, NEW_TOKENS, :], in1=weight[:, 1, :], op=MULT
                )
            for tile_i in range(TOKEN_TILES):
                norm_and_rotate(k_acc[tile_i], tile_i, k_res[tile_i])

            wide_banks = Q_WIDE // N_PASS
            q_acc = [sums.tile([P, N_PASS], F32, name="q_acc%d" % j, tag="acc") for j in range(wide_banks + 1)]
            for g in range(GROUPS):
                words = wide.tile([P, Q_WIDE], U32, name="wide_words", align_bytes=64)
                nc.sync.dma_start(
                    out=words[:].bitcast(I32),
                    in_=Wq_words[g].rearrange("p n t -> p (n t)")[:, 0 : 4 * Q_WIDE].bitcast(I32),
                )
                for j in range(wide_banks):
                    columns = slice(N_PASS * j, N_PASS * (j + 1))
                    project(q_acc[j], NEW_TOKENS, g, words[:, columns], q_plane(g, columns))
            for a in range(GROUPS // SHARE):
                words = narrow.tile([P, SHARE, N_PASS], U32, name="words", tag="narrow", align_bytes=64)
                for i in range(SHARE):
                    g = SHARE * a + i
                    nc.sync.dma_start(
                        out=words[:, i, :].bitcast(I32),
                        in_=Wq_words[g, :, Q_WIDE : HEADS * D, :].rearrange("p n t -> p (n t)").bitcast(I32),
                    )
                    project(q_acc[wide_banks], NEW_TOKENS, g, words[:, i, :], q_plane(g, slice(Q_WIDE, HEADS * D)))
            for out, context, new in ((out_v, v_context, v_new), (out_k, k_context, k_new)):
                store_context(out, context)
                store_new_tokens(out, slice(0, KV_HEADS), CTX, new)
            wide_heads = HEADS_PER_BANK * wide_banks
            q_wide = results.tile([P, wide_heads, D], F32)
            q_last = results.tile([P, HEADS_PER_BANK, D], F32)
            for j in range(wide_banks):
                norm_and_rotate(q_acc[j], TOKEN_TILES, q_wide[:, HEADS_PER_BANK * j : HEADS_PER_BANK * (j + 1), :])
            store_new_tokens(out_q, slice(0, wide_heads), 0, q_wide)
            norm_and_rotate(q_acc[wide_banks], TOKEN_TILES, q_last[:])
            store_new_tokens(out_q, slice(wide_heads, HEADS), 0, q_last)
